import numpy as np
import ml_dtypes


def mxq(x, axis, fmt="e4m3"):
    dtype, down = {"e4m3": (ml_dtypes.float8_e4m3fn, 7), "e5m2": (ml_dtypes.float8_e5m2, 14)}[fmt]
    v = np.moveaxis(np.asarray(x, np.float32).astype(ml_dtypes.bfloat16).astype(np.float64), axis, -1)
    blocks = v.reshape(v.shape[:-1] + (-1, 32))
    amax = np.abs(blocks).max(-1, keepdims=True)
    byte = np.maximum(np.where(amax > 0, np.frexp(amax)[1] - 1 + 127, 0) - down, 1)
    scale = np.exp2(byte - 127.0)
    codes = (blocks / scale).astype(np.float32).astype(dtype).astype(np.float64)
    return np.moveaxis((codes * scale).reshape(v.shape), -1, axis)


WIDE = False


def mx_kscale(k):
    if not WIDE:
        return np.ones(k)
    levels = np.array([10, -10, 5, -5, 0])
    if k % 512:
        return np.exp2(np.random.permutation(np.resize(levels, k // 32))).repeat(32)
    a = np.empty((k // 512, 16))
    for p in range(k // 512):
        a[p, :8] = np.random.permutation(np.resize(levels, 8))
        for g in range(8):
            far = levels[np.abs(levels - a[p, g]) >= 10]
            a[p, g + 8] = far[np.random.randint(len(far))]
    return np.exp2(a.ravel()).repeat(32)


BF16 = ml_dtypes.bfloat16


def bf(x):
    return np.asarray(x, np.float32).astype(BF16)


def f64(x):
    return np.asarray(x).astype(np.float64)


E2M1 = np.array([0.0, 0.5, 1.0, 1.5, 2.0, 3.0, 4.0, 6.0, -0.0, -0.5, -1.0, -1.5, -2.0, -3.0, -4.0, -6.0])


def pack_weight(w, fmt):
    k, n = w.shape
    w = f64(bf(w)).reshape(k // 32, 32, n)
    amax = np.abs(w).max(1)
    if fmt == "e4m3":
        byte = np.frexp(amax)[1] - 1 + 127 - 7
    else:
        mant, ex = np.frexp(amax / 6.0)
        byte = np.where(mant > 0.5, ex, ex - 1) + 127
    byte = np.clip(np.where(amax > 0, byte, 1), 1, 254)
    scaled = (w * np.exp2(127.0 - byte)[:, None, :]).reshape(k, n).astype(np.float32)
    by_word = np.ascontiguousarray(scaled.reshape(k // 512, 128, 4, n).transpose(0, 1, 3, 2))
    if fmt == "e4m3":
        words = by_word.astype(ml_dtypes.float8_e4m3fn).view(np.uint8)
    else:
        c = by_word.astype(ml_dtypes.float4_e2m1fn).view(np.uint8) & 0xF
        words = c[..., 0::2] | (c[..., 1::2] << 4)
    return np.ascontiguousarray(words), np.ascontiguousarray(byte.astype(np.uint8).reshape(k // 512, 16, n))


def unpack_weight(words, scales, fmt):
    g, p, n, _ = words.shape
    if fmt == "e4m3":
        vals = np.ascontiguousarray(words).view(ml_dtypes.float8_e4m3fn).astype(np.float64)
    else:
        nib = np.empty((g, p, n, 4), np.uint8)
        nib[..., 0::2] = words & 0xF
        nib[..., 1::2] = words >> 4
        vals = E2M1[nib]
    vals = vals * np.repeat(np.exp2(scales.astype(np.float64) - 127.0), 8, axis=1)[..., None]
    return vals.transpose(0, 1, 3, 2).reshape(g * 512, n)
def pack4(w):
    words, scales = pack_weight(w, "e2m1")
    return words.reshape(words.shape[0], 128, -1), scales


def unpack4(words, scales):
    return unpack_weight(words.reshape(words.shape[0], 128, -1, 2), scales, "e2m1")


B, N, D, F, M1, M2 = 4, 128, 512, 2048, 3, 5
D2 = D + D


def silu(v):
    return v / (1.0 + np.exp(-v))


def draw0():
    s, t = mx_kscale(D), mx_kscale(D2)
    h = bf(np.random.standard_normal((B, N, D)) * t[:D])
    x1 = bf(np.random.standard_normal((B, N, D, M1)) * s[:, None])
    pre1_words, pre1_scales = pack4(np.random.standard_normal((D, D)) / np.sqrt(D) / s[:, None] * t[D:])
    w1_0_words, w1_0_scales = pack4(np.random.standard_normal((D2, F)) / np.sqrt(D2) / t[:, None])
    return {"h": h,
            "x1": x1,
            "pre1_words": pre1_words,
            "pre1_scales": pre1_scales,
            "w1_0_words": w1_0_words,
            "w1_0_scales": w1_0_scales,
            "b1_0": bf(np.random.standard_normal(F) * 0.2)}


def core(h, x1, pre1_words, pre1_scales, w1_0_words, w1_0_scales, b1_0):
    xt = f64(x1).swapaxes(-1, -2).reshape(B * N * M1, D)
    pm = (mxq(xt, 1, "e4m3") @ unpack4(pre1_words, pre1_scales)).reshape(B, N, M1, D)
    inv = np.sqrt(np.sum(pm * pm, axis=-2))
    mlp_in = np.concatenate([f64(h), inv], axis=-1)
    return silu((mxq(mlp_in, 2, "e4m3") @ unpack4(w1_0_words, w1_0_scales)) + f64(b1_0))


def e4m3fn_bytes(y):
    return np.clip(np.asarray(y, np.float64), -448.0, 448.0).astype(np.float32).astype(ml_dtypes.float8_e4m3fn).view(np.uint8)


def e4m3fn_values(b):
    return np.asarray(b, np.uint8).view(ml_dtypes.float8_e4m3fn).astype(np.float64)


def setup_inputs():
    d = draw0()
    x0 = np.asarray(d['x1']).astype(np.float64)
    s = (np.max(np.abs(x0), axis=(0, 1, 3), keepdims=True) / 448.0).astype(np.float32)
    out = {}
    for k, v in d.items():
        if k == 'x1':
            out['x1_bytes'] = e4m3fn_bytes(x0 / s.astype(np.float64))
            out['x1_scale'] = s
        else:
            out[k] = v
    return out


def reference(h, x1_bytes, x1_scale, pre1_words, pre1_scales, w1_0_words, w1_0_scales, b1_0):
    return core(h, e4m3fn_values(x1_bytes) * x1_scale.astype(np.float64), pre1_words, pre1_scales, w1_0_words, w1_0_scales, b1_0)

@@ -1,0 +1,399 @@
+from contextlib import ExitStack
+
+import concourse.mybir as mybir
+from concourse.masks import make_identity
+
+B, N, D, F, M1 = 4, 128, 512, 2048, 3
+FLOPS = 2 * B * N * M1 * D * D + 2 * B * N * 2 * D * F
+
+F32 = mybir.dt.float32
+BF16 = mybir.dt.bfloat16
+U32 = mybir.dt.uint32
+I32 = mybir.dt.int32
+U8 = mybir.dt.uint8
+F8 = mybir.dt.float8_e4m3fn
+FP8X4 = mybir.dt.float8_e4m3fn_x4
+FP4X4 = mybir.dt.float4_e2m1fn_x4
+ACT = mybir.ActivationFunctionType
+ALU = mybir.AluOpType
+
+P = 128
+T4 = 4
+
+
+def tile_equivariantfeedforward_pa_w4_kernel(
+    tc, h, x1_bytes, x1_scale, pre1_words, pre1_scales, w1_0_words, w1_0_scales, b1_0, out
+):
+    nc = tc.nc
+    with ExitStack() as ctx:
+        keep = ctx.enter_context(tc.tile_pool(name="keep", bufs=1))
+        work = ctx.enter_context(tc.tile_pool(name="work", bufs=4))
+        psum = ctx.enter_context(tc.psum_pool(name="psum", bufs=8))
+        ctx.enter_context(tc.manual_schedule())
+
+        one = keep.tile([P, 1], F32, name="one")
+        ident_b = keep.tile([P, P], BF16, name="ident_b")
+        ident_f = keep.tile([P, P], F32, name="ident_f")
+        sc = keep.tile([P, T4], F32, name="sc")
+        pw = keep.tile([P, 2 * D], U8, name="pw", align_bytes=64)
+        ps = keep.tile([P, D], U8, name="ps", align_bytes=64)
+        w = keep.tile([P, 2, 2 * F], U8, name="w", align_bytes=64)
+        ws = keep.tile([P, 2, F], U8, name="ws", align_bytes=64)
+        bias = keep.tile([P, F], BF16, name="bias")
+        hb = keep.tile([P, B, D], BF16, name="hb", align_bytes=64)
+        hs = keep.tile([P, B * P * T4], BF16, name="hs", align_bytes=64)
+        hc = keep.tile([P, B * P], U32, name="hc", align_bytes=64)
+        hsc = keep.tile([P, B * P], U8, name="hsc", align_bytes=64)
+
+        xb = []
+        for i in range(B):
+            xb_i = work.tile([P, D * M1], U8, name="xb_i", align_bytes=64)
+            xb.append(xb_i)
+
+        nc.vector.memset(one[:], 1.0)
+        nc.vector.memset(ps[:].bitcast(I32), 0)
+        make_identity(nc, ident_b[:])
+        nc.gpsimd.memset(ws[:].rearrange("p g n -> p (g n)").bitcast(I32), 0)
+        make_identity(nc, ident_f[:])
+        nc.scalar.activation(out=one[:], in_=one[:], func=ACT.Sqrt)
+
+        def load_x(i):
+            nc.sync.dma_start(out=xb[i][:], in_=x1_bytes[i].rearrange("n d m -> n (d m)"))
+
+        load_x(0)
+        nc.sync.dma_start(out=sc[:], in_=x1_scale.rearrange("a b (p t) c -> p (a b t c)", t=T4))
+        load_x(1)
+        nc.sync.dma_start(out=pw[:].bitcast(I32), in_=pre1_words[0].bitcast(I32))
+        for q in range(4):
+            nc.sync.dma_start(
+                out=ps[32 * q : 32 * q + 4, :].bitcast(I32),
+                in_=pre1_scales[0, 4 * q : 4 * q + 4, :].bitcast(I32),
+            )
+        load_x(2)
+        nc.sync.dma_start(out=hb[:], in_=h.rearrange("b n d -> n b d"))
+        load_x(3)
+        ws_rows = w1_0_scales.bitcast(I32)
+        ws_i32 = ws[:].rearrange("p g n -> p (g n)").bitcast(I32).rearrange("p (g n) -> p g n", g=2)
+        for q in range(4):
+            nc.sync.dma_start(
+                out=ws_i32[32 * q : 32 * q + 4],
+                in_=ws_rows[:, 4 * q : 4 * q + 4, :].rearrange("g q n -> q g n"),
+            )
+        for g in range(2):
+            nc.sync.dma_start(out=w[:, g, :].bitcast(I32), in_=w1_0_words[g].bitcast(I32))
+        nc.sync.dma_start(out=bias[:], in_=b1_0.partition_broadcast(P))
+
+        xw, xt, xtb, xs, xc, xsc, pm, sq, ss, st, inv = {}, {}, {}, {}, {}, {}, {}, {}, {}, {}, {}
+        itp, iv, ic, isc, htp, ob, pre, res = {}, {}, {}, {}, {}, {}, {}, {}
+
+        def widen(i, eng, c0, c1):
+            if i not in xw:
+                xw_i = work.tile([P, D * M1], BF16, name="xw_i", align_bytes=64)
+                xw[i] = xw_i
+            dst = xw[i][:, c0:c1]
+            src = xb[i][:, c0:c1].bitcast(F8)
+            if eng == "s":
+                nc.scalar.copy(out=dst, in_=src)
+            elif eng == "v":
+                nc.vector.tensor_copy(out=dst, in_=src)
+            else:
+                nc.gpsimd.tensor_copy(out=dst, in_=src)
+
+        def turn(i, m):
+            src = xw[i][:].rearrange("p (k t m) -> p t m k", t=T4, m=M1)
+            if (i, m) not in xt:
+                if m < 2:
+                    xa_b = psum.tile([P, 2, T4, P], BF16, name="xa_b", tag="bank")
+                    xtb[i] = xa_b
+                    xt[i, 0], xt[i, 1] = xa_b[:, 0], xa_b[:, 1]
+                else:
+                    xb_b = psum.tile([P, T4, P], BF16, name="xb_b", tag="bank")
+                    xt[i, 2] = xb_b[:]
+            for t in range(T4):
+                nc.tensor.transpose(xt[i, m][:, t, :], src[:, t, m, :], ident_b[:])
+
+        def scale(i, m, n=1):
+            if i not in xs:
+                xs_i = work.tile([P, M1, P * T4], BF16, name="xs_i", align_bytes=64)
+                xs[i] = xs_i
+            if n == 1:
+                nc.vector.tensor_tensor(
+                    out=xs[i][:, m, :].rearrange("p (r t) -> p r t", t=T4),
+                    in0=xt[i, m].rearrange("p t r -> p r t"),
+                    in1=sc[:].unsqueeze(1).to_broadcast([P, P, T4]),
+                    op=ALU.mult,
+                )
+            else:
+                nc.vector.tensor_tensor(
+                    out=xs[i][:, m : m + n, :].rearrange("p m (r t) -> p m r t", t=T4),
+                    in0=xtb[i][:].rearrange("p m t r -> p m r t"),
+                    in1=sc[:].unsqueeze(1).unsqueeze(1).to_broadcast([P, n, P, T4]),
+                    op=ALU.mult,
+                )
+
+        def quant(i, m, n=1):
+            if i not in xc:
+                xc_i = work.tile([P, M1, P], U32, name="xc_i", align_bytes=64)
+                xsc_i = work.tile([P, M1, P], U8, name="xsc_i", align_bytes=64)
+                xc[i], xsc[i] = xc_i, xsc_i
+            nc.vector.quantize_mx(
+                out=xc[i][:, m : m + n, :].rearrange("p m r -> p (m r)").bitcast(FP8X4),
+                scales=xsc[i][:, m : m + n, :].rearrange("p m r -> p (m r)"),
+                in_=xs[i][:, m : m + n, :].rearrange("p m r -> p (m r)"),
+            )
+
+        def mm1(i, m):
+            pm_b = psum.tile([P, D], F32, name="pm_b", tag="bank")
+            pm[i, m] = pm_b
+            nc.tensor.matmul_mx(
+                out=pm_b[:],
+                lhsT=xc[i][:, m, :].bitcast(FP8X4),
+                lhsT_scale=xsc[i][:, m, :],
+                rhs=pw[:].bitcast(FP4X4),
+                rhs_scale=ps[:],
+                start=True,
+                stop=True,
+            )
+
+        def square(i, m, c0=0, c1=D):
+            if i not in sq:
+                sq_i = work.tile([P, M1, D], F32, name="sq_i")
+                sq[i] = sq_i
+            nc.scalar.activation(out=sq[i][:, m, c0:c1], in_=pm[i, m][:, c0:c1], func=ACT.Square)
+
+        def add01(i, eng):
+            ss_i = work.tile([P, D], F32, name="ss_i")
+            ss[i] = ss_i
+            eng.tensor_tensor(out=ss_i[:], in0=sq[i][:, 0, :], in1=sq[i][:, 1, :], op=ALU.add)
+
+        def add2(i, eng, c0=0, c1=D):
+            if i not in st:
+                st_i = work.tile([P, D], F32, name="st_i")
+                st[i] = st_i
+            eng.tensor_tensor(out=st[i][:, c0:c1], in0=ss[i][:, c0:c1], in1=sq[i][:, 2, c0:c1], op=ALU.add)
+
+        def root(i, c0=0, c1=D):
+            if i not in inv:
+                inv_i = work.tile([P, D], BF16, name="inv_i", align_bytes=64)
+                inv[i] = inv_i
+            nc.scalar.activation(out=inv[i][:, c0:c1], in_=st[i][:, c0:c1], func=ACT.Sqrt)
+
+        def turn_inv(i):
+            words = inv[i][:].bitcast(F32)
+            it_b = psum.tile([P, 2, P], F32, name="it_b", tag="bank")
+            itp[i] = it_b
+            for u in range(2):
+                nc.tensor.transpose(it_b[:, u, :], words[:, u : 256 : 2], ident_f[:])
+
+        def empty_inv(i, eng):
+            iv_i = work.tile([P, P * T4], BF16, name="iv_i", align_bytes=64)
+            iv[i] = iv_i
+            dst = iv_i[:].bitcast(F32).rearrange("p (r u) -> p r u", u=2)
+            src = itp[i][:].rearrange("p u r -> p r u")
+            if eng == "s":
+                nc.scalar.copy(out=dst, in_=src)
+            else:
+                nc.vector.tensor_copy(out=dst, in_=src)
+
+        def quant_inv(i):
+            ic_i = work.tile([P, P], U32, name="ic_i", align_bytes=64)
+            isc_i = work.tile([P, P], U8, name="isc_i", align_bytes=64)
+            ic[i], isc[i] = ic_i, isc_i
+            nc.vector.quantize_mx(out=ic_i[:].bitcast(FP8X4), scales=isc_i[:], in_=iv[i][:])
+
+        def turn_h(j):
+            words = hb[:].rearrange("p b d -> p (b d)").bitcast(F32)
+            ht_b = psum.tile([P, 2, 2, P], F32, name="ht_b", tag="bank")
+            htp[j] = ht_b
+            for a in range(2):
+                i = 2 * j + a
+                for u in range(2):
+                    nc.tensor.transpose(
+                        ht_b[:, a, u, :], words[:, 256 * i + u : 256 * (i + 1) : 2], ident_f[:]
+                    )
+
+        def empty_h(j, eng):
+            dst = hs[:, 1024 * j : 1024 * (j + 1)].bitcast(F32).rearrange("p (a r u) -> p a r u", a=2, u=2)
+            src = htp[j][:].rearrange("p a u r -> p a r u")
+            if eng == "s":
+                nc.scalar.copy(out=dst, in_=src)
+            else:
+                nc.vector.tensor_copy(out=dst, in_=src)
+
+        def quant_h(j):
+            nc.vector.quantize_mx(
+                out=hc[:, 256 * j : 256 * (j + 1)].bitcast(FP8X4),
+                scales=hsc[:, 256 * j : 256 * (j + 1)],
+                in_=hs[:, 1024 * j : 1024 * (j + 1)],
+            )
+
+        def mm2(i, f):
+            ob_b = psum.tile([P, 512], F32, name="ob_b", tag="bank")
+            ob[i, f] = ob_b
+            for g in range(2):
+                if g == 0:
+                    codes, scl = hc[:, P * i : P * (i + 1)], hsc[:, P * i : P * (i + 1)]
+                else:
+                    codes, scl = ic[i][:], isc[i][:]
+                nc.tensor.matmul_mx(
+                    out=ob_b[:],
+                    lhsT=codes.bitcast(FP8X4),
+                    lhsT_scale=scl,
+                    rhs=w[:, g, 1024 * f : 1024 * (f + 1)].bitcast(FP4X4),
+                    rhs_scale=ws[:, g, 512 * f : 512 * (f + 1)],
+                    start=(g == 0),
+                    stop=(g == 1),
+                )
+
+        def add_bias(i, f):
+            if i not in pre:
+                pre_i = work.tile([P, F], F32, name="pre_i")
+                pre[i] = pre_i
+            nc.vector.tensor_tensor(
+                out=pre[i][:, 512 * f : 512 * (f + 1)],
+                in0=ob[i, f][:],
+                in1=bias[:, 512 * f : 512 * (f + 1)],
+                op=ALU.add,
+            )
+
+        def silu_store(i, c0, c1):
+            if i not in res:
+                res_i = work.tile([P, F], F32, name="res_i")
+                res[i] = res_i
+            nc.scalar.activation(out=res[i][:, c0:c1], in_=pre[i][:, c0:c1], func=ACT.Silu)
+            nc.sync.dma_start(out=out[i][:, c0:c1], in_=res[i][:, c0:c1])
+
+        V, G = nc.vector, nc.gpsimd
+        widen(0, "s", 0, 768)
+        widen(0, "v", 768, 1536)
+        turn(0, 0)
+        widen(1, "s", 0, 1536)
+        turn(0, 2)
+        scale(0, 0)
+        turn(0, 1)
+        scale(0, 1)
+        turn_h(0)
+        widen(2, "s", 0, 1536)
+        quant(0, 0)
+        turn(1, 0)
+        quant(0, 1)
+        scale(0, 2)
+        turn(1, 1)
+        turn(1, 2)
+        scale(1, 0, 2)
+        widen(3, "s", 0, 1536)
+        turn(2, 1)
+        scale(1, 2)
+        turn(2, 0)
+        mm1(0, 1)
+        quant(1, 0, 2)
+        mm1(0, 0)
+        scale(2, 0, 2)
+        square(0, 1)
+        turn(3, 0)
+        turn(3, 1)
+        empty_h(0, "s")
+        quant(1, 2)
+        quant(0, 2)
+        square(0, 0)
+        mm1(1, 2)
+        scale(3, 0, 2)
+        mm1(1, 1)
+        square(1, 2)
+        mm1(0, 2)
+        mm1(1, 0)
+        square(0, 2)
+        add01(0, V)
+        turn(3, 2)
+        turn(2, 2)
+        square(1, 0)
+        quant(3, 0, 2)
+        add2(0, V)
+        mm1(3, 1)
+        square(1, 1)
+        turn_h(1)
+        quant(2, 0, 2)
+        root(0)
+        scale(3, 2)
+        mm1(3, 0)
+        empty_h(1, "s")
+        scale(2, 2)
+        mm1(2, 0)
+        turn_inv(0)
+        square(3, 0)
+        add01(1, V)
+        mm1(2, 1)
+        empty_inv(0, "s")
+        quant(2, 2)
+        quant_h(0)
+        square(3, 1)
+        quant(3, 2)
+        quant_inv(0)
+        square(2, 0)
+        add2(1, V)
+        mm2(0, 0)
+        square(2, 1)
+        add01(3, G)
+        mm1(2, 2)
+        add_bias(0, 0)
+        mm1(3, 2)
+        root(1)
+        square(3, 2, 256, 512)
+        add01(2, V)
+        turn_inv(1)
+        square(3, 2, 0, 256)
+        mm2(0, 3)
+        square(2, 2)
+        add2(3, V, 256, 512)
+        add2(3, V, 0, 256)
+        mm2(0, 1)
+        empty_inv(1, "s")
+        add2(2, V)
+        root(3, 256, 512)
+        mm2(0, 2)
+        root(3, 0, 256)
+        quant_inv(1)
+        root(2)
+        add_bias(0, 3)
+        turn_inv(3)
+        mm2(1, 1)
+        empty_inv(3, "v")
+        quant_h(1)
+        mm2(1, 0)
+        quant_inv(3)
+        add_bias(0, 2)
+        mm2(1, 3)
+        add_bias(1, 1)
+        turn_inv(2)
+        add_bias(0, 1)
+        silu_store(0, 1024, 2048)
+        mm2(1, 2)
+        empty_inv(2, "v")
+        mm2(3, 2)
+        add_bias(1, 0)
+        silu_store(0, 0, 1024)
+        quant_inv(2)
+        add_bias(1, 2)
+        mm2(2, 1)
+        add_bias(1, 3)
+        silu_store(1, 0, 1024)
+        mm2(2, 0)
+        mm2(2, 2)
+        add_bias(2, 0)
+        silu_store(1, 1024, 2048)
+        mm2(3, 1)
+        add_bias(2, 1)
+        mm2(2, 3)
+        add_bias(2, 2)
+        silu_store(2, 0, 1024)
+        mm2(3, 3)
+        add_bias(2, 3)
+        mm2(3, 0)
+        add_bias(3, 1)
+        silu_store(2, 1024, 2048)
+        add_bias(3, 0)
+        add_bias(3, 2)
+        silu_store(3, 0, 1024)
+        add_bias(3, 3)
+        silu_store(3, 1024, 1792)
+        silu_store(3, 1792, 2048)

@@ -70,8 +70,10 @@ def tile_equivariantfeedforward_pa_w4_kernel(
                 in_=pre1_scales[0, 4 * q : 4 * q + 4, :].bitcast(I32),
             )
         load_x(2)
-        nc.sync.dma_start(out=hb[:], in_=h.rearrange("b n d -> n b d"))
         load_x(3)
+        nc.sync.dma_start(out=hb[:], in_=h.rearrange("b n d -> n b d"))
+        for g in range(2):
+            nc.sync.dma_start(out=w[:, g, :].bitcast(I32), in_=w1_0_words[g].bitcast(I32))
         ws_rows = w1_0_scales.bitcast(I32)
         ws_i32 = ws[:].rearrange("p g n -> p (g n)").bitcast(I32).rearrange("p (g n) -> p g n", g=2)
         for q in range(4):
@@ -79,9 +81,6 @@ def tile_equivariantfeedforward_pa_w4_kernel(
                 out=ws_i32[32 * q : 32 * q + 4],
                 in_=ws_rows[:, 4 * q : 4 * q + 4, :].rearrange("g q n -> q g n"),
             )
-        for g in range(2):
-            nc.sync.dma_start(out=w[:, g, :].bitcast(I32), in_=w1_0_words[g].bitcast(I32))
-        nc.sync.dma_start(out=bias[:], in_=b1_0.partition_broadcast(P))
 
         xw, xt, xtb, xs, xc, xsc, pm, sq, ss, st, inv = {}, {}, {}, {}, {}, {}, {}, {}, {}, {}, {}
         itp, iv, ic, isc, htp, ob, pre, res = {}, {}, {}, {}, {}, {}, {}, {}
@@ -263,132 +262,136 @@ def tile_equivariantfeedforward_pa_w4_kernel(
             nc.scalar.activation(out=res[i][:, c0:c1], in_=pre[i][:, c0:c1], func=ACT.Silu)
             nc.sync.dma_start(out=out[i][:, c0:c1], in_=res[i][:, c0:c1])
 
+        def load_bias():
+            nc.scalar.dma_start(out=bias[:], in_=b1_0.partition_broadcast(P))
+
         V, G = nc.vector, nc.gpsimd
-        widen(0, "s", 0, 768)
-        widen(0, "v", 768, 1536)
-        turn(0, 0)
-        widen(1, "s", 0, 1536)
+        widen(0, "s", 0, 512)
+        widen(0, "v", 512, 1536)
         turn(0, 2)
-        scale(0, 0)
-        turn(0, 1)
-        scale(0, 1)
-        turn_h(0)
-        widen(2, "s", 0, 1536)
-        quant(0, 0)
-        turn(1, 0)
-        quant(0, 1)
+        widen(1, "s", 0, 1536)
+        turn(0, 0)
         scale(0, 2)
-        turn(1, 1)
+        turn(0, 1)
+        scale(0, 0)
+        widen(2, "s", 0, 1536)
+        scale(0, 1)
         turn(1, 2)
-        scale(1, 0, 2)
-        widen(3, "s", 0, 1536)
-        turn(2, 1)
-        scale(1, 2)
-        turn(2, 0)
-        mm1(0, 1)
-        quant(1, 0, 2)
-        mm1(0, 0)
-        scale(2, 0, 2)
-        square(0, 1)
-        turn(3, 0)
-        turn(3, 1)
-        empty_h(0, "s")
-        quant(1, 2)
         quant(0, 2)
-        square(0, 0)
-        mm1(1, 2)
-        scale(3, 0, 2)
-        mm1(1, 1)
-        square(1, 2)
+        turn(1, 1)
+        quant(0, 1)
+        scale(1, 2)
+        turn(1, 0)
+        quant(0, 0)
+        widen(3, "s", 0, 1536)
+        load_bias()
+        mm1(0, 1)
+        scale(1, 0, 2)
         mm1(0, 2)
-        mm1(1, 0)
-        square(0, 2)
-        add01(0, V)
-        turn(3, 2)
+        mm1(0, 0)
         turn(2, 2)
-        square(1, 0)
-        quant(3, 0, 2)
-        add2(0, V)
-        mm1(3, 1)
-        square(1, 1)
-        turn_h(1)
-        quant(2, 0, 2)
-        root(0)
-        scale(3, 2)
-        mm1(3, 0)
-        empty_h(1, "s")
+        quant(1, 2)
+        square(0, 2)
+        quant(1, 0, 2)
+        turn(2, 1)
         scale(2, 2)
-        mm1(2, 0)
-        turn_inv(0)
-        square(3, 0)
-        add01(1, V)
-        mm1(2, 1)
-        empty_inv(0, "s")
+        square(0, 1)
+        turn(2, 0)
+        square(0, 0)
+        turn_h(1)
         quant(2, 2)
+        scale(2, 0, 2)
+        mm1(1, 1)
+        empty_h(1, "s")
+        mm1(1, 0)
+        add01(0, V)
+        square(1, 1)
+        turn_h(0)
+        turn(3, 1)
+        quant(2, 0, 2)
+        square(1, 0)
+        add2(0, V)
+        turn(3, 0)
+        empty_h(0, "s")
+        add01(1, V)
+        mm1(1, 2)
+        root(0)
+        mm1(2, 0)
+        scale(3, 0, 2)
+        mm1(2, 2)
+        square(1, 2)
+        mm1(2, 1)
+        square(2, 2)
+        turn(3, 2)
         quant_h(0)
-        square(3, 1)
-        quant(3, 2)
-        quant_inv(0)
+        square(2, 1)
+        quant(3, 0, 2)
+        turn_inv(0)
+        scale(3, 2)
+        empty_inv(0, "s")
+        mm1(3, 0)
+        mm1(3, 1)
         square(2, 0)
         add2(1, V)
-        mm2(0, 0)
-        square(2, 1)
-        add01(3, G)
-        mm1(2, 2)
-        add_bias(0, 0)
-        mm1(3, 2)
-        root(1)
-        square(3, 2, 256, 512)
+        square(3, 0)
+        quant_inv(0)
         add01(2, V)
-        turn_inv(1)
-        square(3, 2, 0, 256)
         mm2(0, 3)
-        square(2, 2)
-        add2(3, V, 256, 512)
-        add2(3, V, 0, 256)
-        mm2(0, 1)
-        empty_inv(1, "s")
+        square(3, 1)
+        quant(3, 2)
         add2(2, V)
-        root(3, 256, 512)
-        mm2(0, 2)
-        root(3, 0, 256)
-        quant_inv(1)
-        root(2)
+        root(1)
+        mm1(3, 2)
+        mm2(0, 1)
+        add01(3, G)
         add_bias(0, 3)
+        root(2)
+        turn_inv(1)
+        add_bias(0, 1)
+        square(3, 2, 0, 256)
+        mm2(0, 2)
+        square(3, 2, 256, 512)
+        add2(3, V, 0, 256)
+        empty_inv(1, "s")
+        mm2(0, 0)
+        add2(3, V, 256, 512)
+        root(3, 0, 256)
+        add_bias(0, 2)
+        root(3, 256, 512)
+        turn_inv(2)
+        quant_inv(1)
         turn_inv(3)
         mm2(1, 1)
         empty_inv(3, "v")
-        quant_h(1)
-        mm2(1, 0)
-        quant_inv(3)
-        add_bias(0, 2)
-        mm2(1, 3)
-        add_bias(1, 1)
-        turn_inv(2)
-        add_bias(0, 1)
-        silu_store(0, 1024, 2048)
-        mm2(1, 2)
         empty_inv(2, "v")
-        mm2(3, 2)
-        add_bias(1, 0)
-        silu_store(0, 0, 1024)
+        mm2(1, 0)
+        add_bias(0, 0)
+        mm2(1, 2)
         quant_inv(2)
+        quant_inv(3)
+        silu_store(0, 1024, 2048)
+        quant_h(1)
+        mm2(1, 3)
         add_bias(1, 2)
-        mm2(2, 1)
-        add_bias(1, 3)
-        silu_store(1, 0, 1024)
-        mm2(2, 0)
         mm2(2, 2)
-        add_bias(2, 0)
+        add_bias(1, 3)
+        silu_store(0, 0, 1024)
+        mm2(2, 0)
+        add_bias(1, 1)
+        mm2(2, 1)
         silu_store(1, 1024, 2048)
-        mm2(3, 1)
+        add_bias(1, 0)
+        mm2(3, 3)
         add_bias(2, 1)
         mm2(2, 3)
-        add_bias(2, 2)
-        silu_store(2, 0, 1024)
-        mm2(3, 3)
-        add_bias(2, 3)
+        silu_store(1, 0, 1024)
+        add_bias(2, 0)
         mm2(3, 0)
+        add_bias(2, 3)
+        mm2(3, 1)
+        silu_store(2, 0, 1024)
+        add_bias(2, 2)
+        mm2(3, 2)
         add_bias(3, 1)
         silu_store(2, 1024, 2048)
         add_bias(3, 0)

@@ -219,12 +219,8 @@ def tile_equivariantfeedforward_pa_w4_kernel(
             else:
                 nc.vector.tensor_copy(out=dst, in_=src)
 
-        def quant_h(j):
-            nc.vector.quantize_mx(
-                out=hc[:, 256 * j : 256 * (j + 1)].bitcast(FP8X4),
-                scales=hsc[:, 256 * j : 256 * (j + 1)],
-                in_=hs[:, 1024 * j : 1024 * (j + 1)],
-            )
+        def quant_h():
+            nc.vector.quantize_mx(out=hc[:].bitcast(FP8X4), scales=hsc[:], in_=hs[:])
 
         def mm2(i, f):
             ob_b = psum.tile([P, 512], F32, name="ob_b", tag="bank")
@@ -268,135 +264,130 @@ def tile_equivariantfeedforward_pa_w4_kernel(
         V, G = nc.vector, nc.gpsimd
         widen(0, "s", 0, 512)
         widen(0, "v", 512, 1536)
-        turn(0, 2)
         widen(1, "s", 0, 1536)
+        turn(0, 2)
         turn(0, 0)
-        scale(0, 2)
         turn(0, 1)
-        scale(0, 0)
-        widen(2, "s", 0, 1536)
-        scale(0, 1)
-        turn(1, 2)
-        quant(0, 2)
-        turn(1, 1)
-        quant(0, 1)
-        scale(1, 2)
-        turn(1, 0)
-        quant(0, 0)
+        scale(0, 2)
         widen(3, "s", 0, 1536)
-        load_bias()
-        mm1(0, 1)
-        scale(1, 0, 2)
-        mm1(0, 2)
-        mm1(0, 0)
-        turn(2, 2)
-        quant(1, 2)
-        square(0, 2)
-        quant(1, 0, 2)
-        turn(2, 1)
-        scale(2, 2)
-        square(0, 1)
-        turn(2, 0)
-        square(0, 0)
-        turn_h(1)
-        quant(2, 2)
-        scale(2, 0, 2)
-        mm1(1, 1)
-        empty_h(1, "s")
-        mm1(1, 0)
-        add01(0, V)
-        square(1, 1)
+        quant(0, 2)
+        turn(1, 0)
+        turn(1, 1)
+        scale(0, 0, 2)
         turn_h(0)
-        turn(3, 1)
-        quant(2, 0, 2)
-        square(1, 0)
-        add2(0, V)
+        scale(1, 0, 2)
+        widen(2, "s", 0, 1536)
+        load_bias()
+        turn(1, 2)
         turn(3, 0)
+        turn(3, 1)
+        quant(0, 0, 2)
+        quant(1, 0, 2)
         empty_h(0, "s")
-        add01(1, V)
-        mm1(1, 2)
-        root(0)
-        mm1(2, 0)
+        mm1(0, 0)
         scale(3, 0, 2)
-        mm1(2, 2)
-        square(1, 2)
-        mm1(2, 1)
-        square(2, 2)
-        turn(3, 2)
-        quant_h(0)
-        square(2, 1)
+        mm1(1, 0)
+        square(0, 0)
+        mm1(0, 1)
+        mm1(1, 1)
+        square(0, 1)
+        scale(1, 2)
+        turn(2, 0)
+        turn(2, 1)
+        square(1, 1)
         quant(3, 0, 2)
-        turn_inv(0)
-        scale(3, 2)
-        empty_inv(0, "s")
-        mm1(3, 0)
+        quant(1, 2)
+        mm1(0, 2)
+        square(1, 0)
+        add01(0, G)
+        scale(2, 0, 2)
+        mm1(1, 2)
         mm1(3, 1)
-        square(2, 0)
-        add2(1, V)
-        square(3, 0)
-        quant_inv(0)
-        add01(2, V)
-        mm2(0, 3)
+        square(0, 2)
+        mm1(3, 0)
+        turn(2, 2)
+        square(1, 2)
+        add01(1, V)
+        turn_h(1)
         square(3, 1)
+        quant(2, 0, 2)
+        turn(3, 2)
+        scale(2, 2)
+        add2(0, G)
+        empty_h(1, "s")
+        mm1(2, 0)
+        scale(3, 2)
+        square(3, 0)
+        mm1(2, 1)
+        quant(2, 2)
+        root(0)
         quant(3, 2)
-        add2(2, V)
-        root(1)
+        add01(3, V)
+        square(2, 1)
+        turn_inv(0)
+        quant_h()
         mm1(3, 2)
-        mm2(0, 1)
-        add01(3, G)
-        add_bias(0, 3)
-        root(2)
-        turn_inv(1)
-        add_bias(0, 1)
-        square(3, 2, 0, 256)
-        mm2(0, 2)
-        square(3, 2, 256, 512)
-        add2(3, V, 0, 256)
-        empty_inv(1, "s")
+        empty_inv(0, "s")
+        mm1(2, 2)
+        add2(1, V)
+        square(2, 0)
+        quant_inv(0)
+        square(3, 2)
+        add01(2, V)
         mm2(0, 0)
-        add2(3, V, 256, 512)
-        root(3, 0, 256)
-        add_bias(0, 2)
-        root(3, 256, 512)
-        turn_inv(2)
-        quant_inv(1)
-        turn_inv(3)
-        mm2(1, 1)
-        empty_inv(3, "v")
-        empty_inv(2, "v")
-        mm2(1, 0)
+        square(2, 2)
+        add2(3, V)
+        mm2(0, 1)
+        root(1)
+        add2(2, V)
+        mm2(0, 2)
+        root(3)
+        add_bias(0, 1)
+        turn_inv(1)
+        root(2)
         add_bias(0, 0)
-        mm2(1, 2)
-        quant_inv(2)
+        turn_inv(3)
+        mm2(0, 3)
+        empty_inv(1, "s")
+        empty_inv(3, "v")
+        quant_inv(1)
+        add_bias(0, 2)
+        mm2(1, 1)
+        add_bias(0, 3)
+        turn_inv(2)
         quant_inv(3)
-        silu_store(0, 1024, 2048)
-        quant_h(1)
-        mm2(1, 3)
-        add_bias(1, 2)
-        mm2(2, 2)
-        add_bias(1, 3)
-        silu_store(0, 0, 1024)
-        mm2(2, 0)
+        mm2(1, 0)
+        silu_store(0, 0, 512)
         add_bias(1, 1)
-        mm2(2, 1)
-        silu_store(1, 1024, 2048)
+        mm2(1, 2)
+        silu_store(0, 512, 1024)
         add_bias(1, 0)
+        mm2(1, 3)
+        silu_store(0, 1024, 2048)
+        empty_inv(2, "v")
         mm2(3, 3)
-        add_bias(2, 1)
-        mm2(2, 3)
-        silu_store(1, 0, 1024)
-        add_bias(2, 0)
+        add_bias(1, 2)
         mm2(3, 0)
-        add_bias(2, 3)
-        mm2(3, 1)
-        silu_store(2, 0, 1024)
-        add_bias(2, 2)
+        silu_store(1, 0, 1024)
+        add_bias(1, 3)
         mm2(3, 2)
-        add_bias(3, 1)
-        silu_store(2, 1024, 2048)
-        add_bias(3, 0)
-        add_bias(3, 2)
-        silu_store(3, 0, 1024)
         add_bias(3, 3)
-        silu_store(3, 1024, 1792)
-        silu_store(3, 1792, 2048)
+        mm2(3, 1)
+        silu_store(1, 1024, 2048)
+        add_bias(3, 2)
+        quant_inv(2)
+        add_bias(3, 1)
+        silu_store(3, 1024, 2048)
+        mm2(2, 2)
+        add_bias(3, 0)
+        mm2(2, 3)
+        add_bias(2, 2)
+        mm2(2, 1)
+        silu_store(3, 0, 1024)
+        add_bias(2, 3)
+        mm2(2, 0)
+        add_bias(2, 1)
+        silu_store(2, 1024, 2048)
+        add_bias(2, 0)
+        silu_store(2, 0, 768)
+        silu_store(2, 768, 1024)

@@ -32,6 +32,7 @@ def tile_equivariantfeedforward_pa_w4_kernel(
         ctx.enter_context(tc.manual_schedule())
 
         one = keep.tile([P, 1], F32, name="one")
+        warm = keep.tile([P, 1], F32, name="warm")
         ident_b = keep.tile([P, P], BF16, name="ident_b")
         ident_f = keep.tile([P, P], F32, name="ident_f")
         sc = keep.tile([P, T4], F32, name="sc")
@@ -45,32 +46,33 @@ def tile_equivariantfeedforward_pa_w4_kernel(
         hc = keep.tile([P, B * P], U32, name="hc", align_bytes=64)
         hsc = keep.tile([P, B * P], U8, name="hsc", align_bytes=64)
 
-        xb = []
-        for i in range(B):
-            xb_i = work.tile([P, D * M1], U8, name="xb_i", align_bytes=64)
-            xb.append(xb_i)
+        xb_all = keep.tile([P, B, D * M1], U8, name="xb_all", align_bytes=64)
+        xb = [xb_all[:, 0, :], xb_all[:, 1, :], xb_all[:, 2, :], xb_all[:, 3, :]]
 
+        nc.vector.memset(warm[:], 1.0)
         nc.vector.memset(one[:], 1.0)
         nc.vector.memset(ps[:].bitcast(I32), 0)
         make_identity(nc, ident_b[:])
         nc.gpsimd.memset(ws[:].rearrange("p g n -> p (g n)").bitcast(I32), 0)
         make_identity(nc, ident_f[:])
-        nc.scalar.activation(out=one[:], in_=one[:], func=ACT.Sqrt)
+        nc.scalar.activation(out=warm[:], in_=warm[:], func=ACT.Sqrt)
 
-        def load_x(i):
-            nc.sync.dma_start(out=xb[i][:], in_=x1_bytes[i].rearrange("n d m -> n (d m)"))
+        def load_x(i, n):
+            nc.sync.dma_start(
+                out=xb_all[:, i : i + n, :], in_=x1_bytes[i : i + n].rearrange("b n d m -> n b (d m)")
+            )
 
-        load_x(0)
+        load_x(0, 1)
         nc.sync.dma_start(out=sc[:], in_=x1_scale.rearrange("a b (p t) c -> p (a b t c)", t=T4))
-        load_x(1)
+        load_x(1, 1)
+        load_x(2, 1)
+        load_x(3, 1)
         nc.sync.dma_start(out=pw[:].bitcast(I32), in_=pre1_words[0].bitcast(I32))
         for q in range(4):
             nc.sync.dma_start(
                 out=ps[32 * q : 32 * q + 4, :].bitcast(I32),
                 in_=pre1_scales[0, 4 * q : 4 * q + 4, :].bitcast(I32),
             )
-        load_x(2)
-        load_x(3)
         nc.sync.dma_start(out=hb[:], in_=h.rearrange("b n d -> n b d"))
         for g in range(2):
             nc.sync.dma_start(out=w[:, g, :].bitcast(I32), in_=w1_0_words[g].bitcast(I32))
@@ -82,7 +84,7 @@ def tile_equivariantfeedforward_pa_w4_kernel(
                 in_=ws_rows[:, 4 * q : 4 * q + 4, :].rearrange("g q n -> q g n"),
             )
 
-        xw, xt, xtb, xs, xc, xsc, pm, sq, ss, st, inv = {}, {}, {}, {}, {}, {}, {}, {}, {}, {}, {}
+        xv, xw, xt, xtb, xs, xc, xsc, pm, sq, ss, st, inv = {}, {}, {}, {}, {}, {}, {}, {}, {}, {}, {}, {}
         itp, iv, ic, isc, htp, ob, pre, res = {}, {}, {}, {}, {}, {}, {}, {}
 
         def widen(i, eng, c0, c1):
@@ -97,6 +99,40 @@ def tile_equivariantfeedforward_pa_w4_kernel(
                 nc.vector.tensor_copy(out=dst, in_=src)
             else:
                 nc.gpsimd.tensor_copy(out=dst, in_=src)
+
+        def widen_planes(i):
+            xv_i = work.tile([P, M1, D], BF16, name="xv_i", align_bytes=64)
+            xv[i] = xv_i
+            nc.vector.tensor_scalar(
+                out=xv_i[:].rearrange("p m d -> p d m"),
+                in0=xb[i].bitcast(F8).rearrange("p (d m) -> p d m", m=M1),
+                scalar1=one[:],
+                scalar2=None,
+                op0=ALU.mult,
+            )
+
+        def turn_words(i, m):
+            if (i, m) not in xt:
+                if m < 2:
+                    xu_b = psum.tile([P, 2, 2, P], F32, name="xu_b", tag="bank")
+                    xt[i, 0], xt[i, 1] = xu_b[:, 0], xu_b[:, 1]
+                else:
+                    xz_b = psum.tile([P, 2, P], F32, name="xz_b", tag="bank")
+                    xt[i, 2] = xz_b[:]
+            words = xv[i][:, m, :].bitcast(F32)
+            for u in range(2):
+                nc.tensor.transpose(xt[i, m][:, u, :], words[:, u : 256 : 2], ident_f[:])
+
+        def scale_words(i, m):
+            if i not in xs:
+                xs_i = work.tile([P, M1, P * T4], BF16, name="xs_i", align_bytes=64)
+                xs[i] = xs_i
+            nc.vector.tensor_tensor(
+                out=xs[i][:, m, :].rearrange("p (r u e) -> p r u e", u=2, e=2),
+                in0=xt[i, m].rearrange("p u r -> p (u r)").bitcast(BF16).rearrange("p (u r e) -> p r u e", u=2, e=2),
+                in1=sc[:].rearrange("p (u e) -> p u e", u=2).unsqueeze(1).to_broadcast([P, P, 2, 2]),
+                op=ALU.mult,
+            )
 
         def turn(i, m):
             src = xw[i][:].rearrange("p (k t m) -> p t m k", t=T4, m=M1)
@@ -262,132 +298,133 @@ def tile_equivariantfeedforward_pa_w4_kernel(
             nc.scalar.dma_start(out=bias[:], in_=b1_0.partition_broadcast(P))
 
         V, G = nc.vector, nc.gpsimd
-        widen(0, "s", 0, 512)
-        widen(0, "v", 512, 1536)
+        widen_planes(0)
         widen(1, "s", 0, 1536)
-        turn(0, 2)
-        turn(0, 0)
-        turn(0, 1)
-        scale(0, 2)
+        turn_words(0, 0)
+        turn_words(0, 1)
+        widen_planes(2)
+        turn_words(0, 2)
         widen(3, "s", 0, 1536)
-        quant(0, 2)
         turn(1, 0)
         turn(1, 1)
-        scale(0, 0, 2)
-        turn_h(0)
-        scale(1, 0, 2)
-        widen(2, "s", 0, 1536)
-        load_bias()
-        turn(1, 2)
+        scale_words(0, 0)
+        scale_words(0, 1)
+        turn_words(2, 0)
+        turn_words(2, 1)
+        scale_words(0, 2)
+        turn_h(1)
+        quant(0, 0, 2)
+        scale_words(2, 1)
+        mm1(0, 1)
+        mm1(0, 0)
+        scale_words(2, 0)
+        square(0, 1)
+        turn_words(2, 2)
         turn(3, 0)
         turn(3, 1)
-        quant(0, 0, 2)
-        quant(1, 0, 2)
-        empty_h(0, "s")
-        mm1(0, 0)
-        scale(3, 0, 2)
-        mm1(1, 0)
+        quant(0, 2)
         square(0, 0)
-        mm1(0, 1)
-        mm1(1, 1)
-        square(0, 1)
-        scale(1, 2)
-        turn(2, 0)
-        turn(2, 1)
-        square(1, 1)
-        quant(3, 0, 2)
-        quant(1, 2)
-        mm1(0, 2)
-        square(1, 0)
-        add01(0, G)
-        scale(2, 0, 2)
-        mm1(1, 2)
-        mm1(3, 1)
-        square(0, 2)
-        mm1(3, 0)
-        turn(2, 2)
-        square(1, 2)
-        add01(1, V)
-        turn_h(1)
-        square(3, 1)
         quant(2, 0, 2)
-        turn(3, 2)
-        scale(2, 2)
-        add2(0, G)
+        scale(1, 0, 2)
         empty_h(1, "s")
-        mm1(2, 0)
-        scale(3, 2)
-        square(3, 0)
+        add01(0, G)
+        mm1(0, 2)
+        square(0, 2)
+        load_bias()
+        scale_words(2, 2)
         mm1(2, 1)
+        mm1(2, 0)
+        quant(1, 0, 2)
+        square(2, 1)
+        turn(3, 2)
+        scale(3, 0, 2)
+        add2(0, G)
+        square(2, 0)
+        turn_h(0)
+        scale(3, 2)
+        mm1(1, 0)
+        empty_h(0, "s")
+        turn(1, 2)
         quant(2, 2)
         root(0)
-        quant(3, 2)
-        add01(3, V)
-        square(2, 1)
-        turn_inv(0)
-        quant_h()
-        mm1(3, 2)
-        empty_inv(0, "s")
-        mm1(2, 2)
-        add2(1, V)
-        square(2, 0)
-        quant_inv(0)
-        square(3, 2)
+        quant(3, 0, 2)
+        mm1(1, 1)
         add01(2, V)
-        mm2(0, 0)
+        square(1, 0)
+        turn_inv(0)
+        quant(3, 2)
+        square(1, 1)
+        mm1(2, 2)
+        scale(1, 2)
+        mm1(3, 1)
+        empty_inv(0, "s")
+        mm1(3, 0)
+        quant_h()
         square(2, 2)
-        add2(3, V)
-        mm2(0, 1)
-        root(1)
+        quant(1, 2)
+        square(3, 1)
+        add01(1, V)
+        mm1(1, 2)
+        square(3, 0)
+        mm1(3, 2)
+        quant_inv(0)
         add2(2, V)
-        mm2(0, 2)
-        root(3)
-        add_bias(0, 1)
-        turn_inv(1)
-        root(2)
-        add_bias(0, 0)
-        turn_inv(3)
+        mm2(0, 0)
+        square(1, 2)
+        add01(3, V)
+        mm2(0, 1)
+        square(3, 2)
+        add2(1, V)
         mm2(0, 3)
-        empty_inv(1, "s")
-        empty_inv(3, "v")
-        quant_inv(1)
-        add_bias(0, 2)
-        mm2(1, 1)
-        add_bias(0, 3)
+        root(2)
+        add2(3, V)
+        mm2(0, 2)
+        root(1)
+        add_bias(0, 0)
         turn_inv(2)
-        quant_inv(3)
-        mm2(1, 0)
-        silu_store(0, 0, 512)
-        add_bias(1, 1)
-        mm2(1, 2)
-        silu_store(0, 512, 1024)
-        add_bias(1, 0)
-        mm2(1, 3)
-        silu_store(0, 1024, 2048)
-        empty_inv(2, "v")
-        mm2(3, 3)
-        add_bias(1, 2)
-        mm2(3, 0)
-        silu_store(1, 0, 1024)
-        add_bias(1, 3)
-        mm2(3, 2)
-        add_bias(3, 3)
-        mm2(3, 1)
-        silu_store(1, 1024, 2048)
-        add_bias(3, 2)
+        root(3)
+        turn_inv(1)
+        add_bias(0, 3)
+        empty_inv(2, "s")
+        turn_inv(3)
+        add_bias(0, 1)
         quant_inv(2)
-        add_bias(3, 1)
-        silu_store(3, 1024, 2048)
+        add_bias(0, 2)
         mm2(2, 2)
-        add_bias(3, 0)
-        mm2(2, 3)
-        add_bias(2, 2)
-        mm2(2, 1)
-        silu_store(3, 0, 1024)
-        add_bias(2, 3)
+        empty_inv(3, "v")
         mm2(2, 0)
+        empty_inv(1, "s")
+        add_bias(2, 2)
+        silu_store(0, 0, 512)
+        mm2(2, 3)
+        quant_inv(3)
+        silu_store(0, 512, 1024)
+        quant_inv(1)
+        mm2(2, 1)
+        add_bias(2, 3)
+        silu_store(0, 1024, 2048)
+        mm2(1, 3)
+        add_bias(2, 0)
+        mm2(1, 0)
         add_bias(2, 1)
         silu_store(2, 1024, 2048)
-        add_bias(2, 0)
-        silu_store(2, 0, 768)
-        silu_store(2, 768, 1024)
+        mm2(1, 1)
+        add_bias(1, 0)
+        mm2(3, 2)
+        silu_store(2, 0, 1024)
+        add_bias(1, 1)
+        mm2(1, 2)
+        add_bias(1, 3)
+        mm2(3, 3)
+        silu_store(1, 0, 1024)
+        add_bias(1, 2)
+        mm2(3, 1)
+        add_bias(3, 3)
+        mm2(3, 0)
+        silu_store(1, 1024, 2048)
+        add_bias(3, 2)
+        add_bias(3, 1)
+        silu_store(3, 1024, 2048)
+        add_bias(3, 0)
+        silu_store(3, 0, 768)
+        silu_store(3, 768, 1024)

from contextlib import ExitStack

import concourse.mybir as mybir
from concourse.masks import make_identity

B, N, D, F, M1 = 4, 128, 512, 2048, 3
FLOPS = 2 * B * N * M1 * D * D + 2 * B * N * 2 * D * F

F32 = mybir.dt.float32
BF16 = mybir.dt.bfloat16
U32 = mybir.dt.uint32
I32 = mybir.dt.int32
U8 = mybir.dt.uint8
F8 = mybir.dt.float8_e4m3fn
FP8X4 = mybir.dt.float8_e4m3fn_x4
FP4X4 = mybir.dt.float4_e2m1fn_x4
ACT = mybir.ActivationFunctionType
ALU = mybir.AluOpType

P = 128
T4 = 4


def tile_equivariantfeedforward_pa_w4_kernel(
    tc, h, x1_bytes, x1_scale, pre1_words, pre1_scales, w1_0_words, w1_0_scales, b1_0, out
):
    nc = tc.nc
    with ExitStack() as ctx:
        keep = ctx.enter_context(tc.tile_pool(name="keep", bufs=1))
        work = ctx.enter_context(tc.tile_pool(name="work", bufs=4))
        psum = ctx.enter_context(tc.psum_pool(name="psum", bufs=8))
        ctx.enter_context(tc.manual_schedule())

        one = keep.tile([P, 1], F32, name="one")
        warm = keep.tile([P, 1], F32, name="warm")
        ident_b = keep.tile([P, P], BF16, name="ident_b")
        ident_f = keep.tile([P, P], F32, name="ident_f")
        sc = keep.tile([P, T4], F32, name="sc")
        pw = keep.tile([P, 2 * D], U8, name="pw", align_bytes=64)
        ps = keep.tile([P, D], U8, name="ps", align_bytes=64)
        w = keep.tile([P, 2, 2 * F], U8, name="w", align_bytes=64)
        ws = keep.tile([P, 2, F], U8, name="ws", align_bytes=64)
        bias = keep.tile([P, F], BF16, name="bias")
        hb = keep.tile([P, B, D], BF16, name="hb", align_bytes=64)
        hs = keep.tile([P, B * P * T4], BF16, name="hs", align_bytes=64)
        hc = keep.tile([P, B * P], U32, name="hc", align_bytes=64)
        hsc = keep.tile([P, B * P], U8, name="hsc", align_bytes=64)

        xb_all = keep.tile([P, B, D * M1], U8, name="xb_all", align_bytes=64)
        xb = [xb_all[:, 0, :], xb_all[:, 1, :], xb_all[:, 2, :], xb_all[:, 3, :]]

        nc.vector.memset(warm[:], 1.0)
        nc.vector.memset(one[:], 1.0)
        nc.vector.memset(ps[:].bitcast(I32), 0)
        make_identity(nc, ident_b[:])
        nc.gpsimd.memset(ws[:].rearrange("p g n -> p (g n)").bitcast(I32), 0)
        make_identity(nc, ident_f[:])
        nc.scalar.activation(out=warm[:], in_=warm[:], func=ACT.Sqrt)

        def load_x(i, n):
            nc.sync.dma_start(
                out=xb_all[:, i : i + n, :], in_=x1_bytes[i : i + n].rearrange("b n d m -> n b (d m)")
            )

        load_x(0, 1)
        nc.sync.dma_start(out=sc[:], in_=x1_scale.rearrange("a b (p t) c -> p (a b t c)", t=T4))
        load_x(1, 1)
        load_x(2, 1)
        load_x(3, 1)
        nc.sync.dma_start(out=pw[:].bitcast(I32), in_=pre1_words[0].bitcast(I32))
        for q in range(4):
            nc.sync.dma_start(
                out=ps[32 * q : 32 * q + 4, :].bitcast(I32),
                in_=pre1_scales[0, 4 * q : 4 * q + 4, :].bitcast(I32),
            )
        nc.sync.dma_start(out=hb[:], in_=h.rearrange("b n d -> n b d"))
        for g in range(2):
            nc.sync.dma_start(out=w[:, g, :].bitcast(I32), in_=w1_0_words[g].bitcast(I32))
        ws_rows = w1_0_scales.bitcast(I32)
        ws_i32 = ws[:].rearrange("p g n -> p (g n)").bitcast(I32).rearrange("p (g n) -> p g n", g=2)
        for q in range(4):
            nc.sync.dma_start(
                out=ws_i32[32 * q : 32 * q + 4],
                in_=ws_rows[:, 4 * q : 4 * q + 4, :].rearrange("g q n -> q g n"),
            )

        xv, xw, xt, xtb, xs, xc, xsc, pm, sq, ss, st, inv = {}, {}, {}, {}, {}, {}, {}, {}, {}, {}, {}, {}
        itp, iv, ic, isc, htp, ob, pre, res = {}, {}, {}, {}, {}, {}, {}, {}

        def widen(i, eng, c0, c1):
            if i not in xw:
                xw_i = work.tile([P, D * M1], BF16, name="xw_i", align_bytes=64)
                xw[i] = xw_i
            dst = xw[i][:, c0:c1]
            src = xb[i][:, c0:c1].bitcast(F8)
            if eng == "s":
                nc.scalar.copy(out=dst, in_=src)
            elif eng == "v":
                nc.vector.tensor_copy(out=dst, in_=src)
            else:
                nc.gpsimd.tensor_copy(out=dst, in_=src)

        def widen_planes(i):
            xv_i = work.tile([P, M1, D], BF16, name="xv_i", align_bytes=64)
            xv[i] = xv_i
            nc.vector.tensor_scalar(
                out=xv_i[:].rearrange("p m d -> p d m"),
                in0=xb[i].bitcast(F8).rearrange("p (d m) -> p d m", m=M1),
                scalar1=one[:],
                scalar2=None,
                op0=ALU.mult,
            )

        def turn_words(i, m):
            if (i, m) not in xt:
                if m < 2:
                    xu_b = psum.tile([P, 2, 2, P], F32, name="xu_b", tag="bank")
                    xt[i, 0], xt[i, 1] = xu_b[:, 0], xu_b[:, 1]
                else:
                    xz_b = psum.tile([P, 2, P], F32, name="xz_b", tag="bank")
                    xt[i, 2] = xz_b[:]
            words = xv[i][:, m, :].bitcast(F32)
            for u in range(2):
                nc.tensor.transpose(xt[i, m][:, u, :], words[:, u : 256 : 2], ident_f[:])

        def scale_words(i, m):
            if i not in xs:
                xs_i = work.tile([P, M1, P * T4], BF16, name="xs_i", align_bytes=64)
                xs[i] = xs_i
            nc.vector.tensor_tensor(
                out=xs[i][:, m, :].rearrange("p (r u e) -> p r u e", u=2, e=2),
                in0=xt[i, m].rearrange("p u r -> p (u r)").bitcast(BF16).rearrange("p (u r e) -> p r u e", u=2, e=2),
                in1=sc[:].rearrange("p (u e) -> p u e", u=2).unsqueeze(1).to_broadcast([P, P, 2, 2]),
                op=ALU.mult,
            )

        def turn(i, m):
            src = xw[i][:].rearrange("p (k t m) -> p t m k", t=T4, m=M1)
            if (i, m) not in xt:
                if m < 2:
                    xa_b = psum.tile([P, 2, T4, P], BF16, name="xa_b", tag="bank")
                    xtb[i] = xa_b
                    xt[i, 0], xt[i, 1] = xa_b[:, 0], xa_b[:, 1]
                else:
                    xb_b = psum.tile([P, T4, P], BF16, name="xb_b", tag="bank")
                    xt[i, 2] = xb_b[:]
            for t in range(T4):
                nc.tensor.transpose(xt[i, m][:, t, :], src[:, t, m, :], ident_b[:])

        def scale(i, m, n=1):
            if i not in xs:
                xs_i = work.tile([P, M1, P * T4], BF16, name="xs_i", align_bytes=64)
                xs[i] = xs_i
            if n == 1:
                nc.vector.tensor_tensor(
                    out=xs[i][:, m, :].rearrange("p (r t) -> p r t", t=T4),
                    in0=xt[i, m].rearrange("p t r -> p r t"),
                    in1=sc[:].unsqueeze(1).to_broadcast([P, P, T4]),
                    op=ALU.mult,
                )
            else:
                nc.vector.tensor_tensor(
                    out=xs[i][:, m : m + n, :].rearrange("p m (r t) -> p m r t", t=T4),
                    in0=xtb[i][:].rearrange("p m t r -> p m r t"),
                    in1=sc[:].unsqueeze(1).unsqueeze(1).to_broadcast([P, n, P, T4]),
                    op=ALU.mult,
                )

        def quant(i, m, n=1):
            if i not in xc:
                xc_i = work.tile([P, M1, P], U32, name="xc_i", align_bytes=64)
                xsc_i = work.tile([P, M1, P], U8, name="xsc_i", align_bytes=64)
                xc[i], xsc[i] = xc_i, xsc_i
            nc.vector.quantize_mx(
                out=xc[i][:, m : m + n, :].rearrange("p m r -> p (m r)").bitcast(FP8X4),
                scales=xsc[i][:, m : m + n, :].rearrange("p m r -> p (m r)"),
                in_=xs[i][:, m : m + n, :].rearrange("p m r -> p (m r)"),
            )

        def mm1(i, m):
            pm_b = psum.tile([P, D], F32, name="pm_b", tag="bank")
            pm[i, m] = pm_b
            nc.tensor.matmul_mx(
                out=pm_b[:],
                lhsT=xc[i][:, m, :].bitcast(FP8X4),
                lhsT_scale=xsc[i][:, m, :],
                rhs=pw[:].bitcast(FP4X4),
                rhs_scale=ps[:],
                start=True,
                stop=True,
            )

        def square(i, m, c0=0, c1=D):
            if i not in sq:
                sq_i = work.tile([P, M1, D], F32, name="sq_i")
                sq[i] = sq_i
            nc.scalar.activation(out=sq[i][:, m, c0:c1], in_=pm[i, m][:, c0:c1], func=ACT.Square)

        def add01(i, eng):
            ss_i = work.tile([P, D], F32, name="ss_i")
            ss[i] = ss_i
            eng.tensor_tensor(out=ss_i[:], in0=sq[i][:, 0, :], in1=sq[i][:, 1, :], op=ALU.add)

        def add2(i, eng, c0=0, c1=D):
            if i not in st:
                st_i = work.tile([P, D], F32, name="st_i")
                st[i] = st_i
            eng.tensor_tensor(out=st[i][:, c0:c1], in0=ss[i][:, c0:c1], in1=sq[i][:, 2, c0:c1], op=ALU.add)

        def root(i, c0=0, c1=D):
            if i not in inv:
                inv_i = work.tile([P, D], BF16, name="inv_i", align_bytes=64)
                inv[i] = inv_i
            nc.scalar.activation(out=inv[i][:, c0:c1], in_=st[i][:, c0:c1], func=ACT.Sqrt)

        def turn_inv(i):
            words = inv[i][:].bitcast(F32)
            it_b = psum.tile([P, 2, P], F32, name="it_b", tag="bank")
            itp[i] = it_b
            for u in range(2):
                nc.tensor.transpose(it_b[:, u, :], words[:, u : 256 : 2], ident_f[:])

        def empty_inv(i, eng):
            iv_i = work.tile([P, P * T4], BF16, name="iv_i", align_bytes=64)
            iv[i] = iv_i
            dst = iv_i[:].bitcast(F32).rearrange("p (r u) -> p r u", u=2)
            src = itp[i][:].rearrange("p u r -> p r u")
            if eng == "s":
                nc.scalar.copy(out=dst, in_=src)
            else:
                nc.vector.tensor_copy(out=dst, in_=src)

        def quant_inv(i):
            ic_i = work.tile([P, P], U32, name="ic_i", align_bytes=64)
            isc_i = work.tile([P, P], U8, name="isc_i", align_bytes=64)
            ic[i], isc[i] = ic_i, isc_i
            nc.vector.quantize_mx(out=ic_i[:].bitcast(FP8X4), scales=isc_i[:], in_=iv[i][:])

        def turn_h(j):
            words = hb[:].rearrange("p b d -> p (b d)").bitcast(F32)
            ht_b = psum.tile([P, 2, 2, P], F32, name="ht_b", tag="bank")
            htp[j] = ht_b
            for a in range(2):
                i = 2 * j + a
                for u in range(2):
                    nc.tensor.transpose(
                        ht_b[:, a, u, :], words[:, 256 * i + u : 256 * (i + 1) : 2], ident_f[:]
                    )

        def empty_h(j, eng):
            dst = hs[:, 1024 * j : 1024 * (j + 1)].bitcast(F32).rearrange("p (a r u) -> p a r u", a=2, u=2)
            src = htp[j][:].rearrange("p a u r -> p a r u")
            if eng == "s":
                nc.scalar.copy(out=dst, in_=src)
            else:
                nc.vector.tensor_copy(out=dst, in_=src)

        def quant_h():
            nc.vector.quantize_mx(out=hc[:].bitcast(FP8X4), scales=hsc[:], in_=hs[:])

        def mm2(i, f):
            ob_b = psum.tile([P, 512], F32, name="ob_b", tag="bank")
            ob[i, f] = ob_b
            for g in range(2):
                if g == 0:
                    codes, scl = hc[:, P * i : P * (i + 1)], hsc[:, P * i : P * (i + 1)]
                else:
                    codes, scl = ic[i][:], isc[i][:]
                nc.tensor.matmul_mx(
                    out=ob_b[:],
                    lhsT=codes.bitcast(FP8X4),
                    lhsT_scale=scl,
                    rhs=w[:, g, 1024 * f : 1024 * (f + 1)].bitcast(FP4X4),
                    rhs_scale=ws[:, g, 512 * f : 512 * (f + 1)],
                    start=(g == 0),
                    stop=(g == 1),
                )

        def add_bias(i, f):
            if i not in pre:
                pre_i = work.tile([P, F], F32, name="pre_i")
                pre[i] = pre_i
            nc.vector.tensor_tensor(
                out=pre[i][:, 512 * f : 512 * (f + 1)],
                in0=ob[i, f][:],
                in1=bias[:, 512 * f : 512 * (f + 1)],
                op=ALU.add,
            )

        def silu_store(i, c0, c1):
            if i not in res:
                res_i = work.tile([P, F], F32, name="res_i")
                res[i] = res_i
            nc.scalar.activation(out=res[i][:, c0:c1], in_=pre[i][:, c0:c1], func=ACT.Silu)
            nc.sync.dma_start(out=out[i][:, c0:c1], in_=res[i][:, c0:c1])

        def load_bias():
            nc.scalar.dma_start(out=bias[:], in_=b1_0.partition_broadcast(P))

        V, G = nc.vector, nc.gpsimd
        widen_planes(0)
        widen(1, "s", 0, 1536)
        turn_words(0, 0)
        turn_words(0, 1)
        widen_planes(2)
        turn_words(0, 2)
        widen(3, "s", 0, 1536)
        turn(1, 0)
        turn(1, 1)
        scale_words(0, 0)
        scale_words(0, 1)
        turn_words(2, 0)
        turn_words(2, 1)
        scale_words(0, 2)
        turn_h(1)
        quant(0, 0, 2)
        scale_words(2, 1)
        mm1(0, 1)
        mm1(0, 0)
        scale_words(2, 0)
        square(0, 1)
        turn_words(2, 2)
        turn(3, 0)
        turn(3, 1)
        quant(0, 2)
        square(0, 0)
        quant(2, 0, 2)
        scale(1, 0, 2)
        empty_h(1, "s")
        add01(0, G)
        mm1(0, 2)
        square(0, 2)
        load_bias()
        scale_words(2, 2)
        mm1(2, 1)
        mm1(2, 0)
        quant(1, 0, 2)
        square(2, 1)
        turn(3, 2)
        scale(3, 0, 2)
        add2(0, G)
        square(2, 0)
        turn_h(0)
        scale(3, 2)
        mm1(1, 0)
        empty_h(0, "s")
        turn(1, 2)
        quant(2, 2)
        root(0)
        quant(3, 0, 2)
        mm1(1, 1)
        add01(2, V)
        square(1, 0)
        turn_inv(0)
        quant(3, 2)
        square(1, 1)
        mm1(2, 2)
        scale(1, 2)
        mm1(3, 1)
        empty_inv(0, "s")
        mm1(3, 0)
        quant_h()
        square(2, 2)
        quant(1, 2)
        square(3, 1)
        add01(1, V)
        mm1(1, 2)
        square(3, 0)
        mm1(3, 2)
        quant_inv(0)
        add2(2, V)
        mm2(0, 0)
        square(1, 2)
        add01(3, V)
        mm2(0, 1)
        square(3, 2)
        add2(1, V)
        mm2(0, 3)
        root(2)
        add2(3, V)
        mm2(0, 2)
        root(1)
        add_bias(0, 0)
        turn_inv(2)
        root(3)
        turn_inv(1)
        add_bias(0, 3)
        empty_inv(2, "s")
        turn_inv(3)
        add_bias(0, 1)
        quant_inv(2)
        add_bias(0, 2)
        mm2(2, 2)
        empty_inv(3, "v")
        mm2(2, 0)
        empty_inv(1, "s")
        add_bias(2, 2)
        silu_store(0, 0, 512)
        mm2(2, 3)
        quant_inv(3)
        silu_store(0, 512, 1024)
        quant_inv(1)
        mm2(2, 1)
        add_bias(2, 3)
        silu_store(0, 1024, 2048)
        mm2(1, 3)
        add_bias(2, 0)
        mm2(1, 0)
        add_bias(2, 1)
        silu_store(2, 1024, 2048)
        mm2(1, 1)
        add_bias(1, 0)
        mm2(3, 2)
        silu_store(2, 0, 1024)
        add_bias(1, 1)
        mm2(1, 2)
        add_bias(1, 3)
        mm2(3, 3)
        silu_store(1, 0, 1024)
        add_bias(1, 2)
        mm2(3, 1)
        add_bias(3, 3)
        mm2(3, 0)
        silu_store(1, 1024, 2048)
        add_bias(3, 2)
        add_bias(3, 1)
        silu_store(3, 1024, 2048)
        add_bias(3, 0)
        silu_store(3, 0, 768)
        silu_store(3, 768, 1024)
